import numpy as np
import ml_dtypes


def mxq(x, axis, fmt="e4m3"):
    dtype, down = {"e4m3": (ml_dtypes.float8_e4m3fn, 7), "e5m2": (ml_dtypes.float8_e5m2, 14)}[fmt]
    v = np.moveaxis(np.asarray(x, np.float32).astype(ml_dtypes.bfloat16).astype(np.float64), axis, -1)
    blocks = v.reshape(v.shape[:-1] + (-1, 32))
    amax = np.abs(blocks).max(-1, keepdims=True)
    byte = np.maximum(np.where(amax > 0, np.frexp(amax)[1] - 1 + 127, 0) - down, 1)
    scale = np.exp2(byte - 127.0)
    codes = (blocks / scale).astype(np.float32).astype(dtype).astype(np.float64)
    return np.moveaxis((codes * scale).reshape(v.shape), -1, axis)


WIDE = False


def mx_kscale(k):
    if not WIDE:
        return np.ones(k)
    levels = np.array([10, -10, 5, -5, 0])
    if k % 512:
        return np.exp2(np.random.permutation(np.resize(levels, k // 32))).repeat(32)
    a = np.empty((k // 512, 16))
    for p in range(k // 512):
        a[p, :8] = np.random.permutation(np.resize(levels, 8))
        for g in range(8):
            far = levels[np.abs(levels - a[p, g]) >= 10]
            a[p, g + 8] = far[np.random.randint(len(far))]
    return np.exp2(a.ravel()).repeat(32)


BF16 = ml_dtypes.bfloat16


def bf(x):
    return np.asarray(x, np.float32).astype(BF16)


def f64(x):
    return np.asarray(x).astype(np.float64)


B, P0, P1, P2, K0, K1, K2 = 4096, 128, 128, 128, 512, 512, 512
PT = P0 + P1 + P2
KT = K0 + K1 + K2
CLIP1 = 1.0


def clip_rows(mat, clip):
    norms = np.sqrt(np.sum(mat * mat, axis=1, keepdims=True))
    scale = np.minimum(clip / norms, 1.0)
    return mat * scale


def setup_inputs():
    t0, t1, t2 = mx_kscale(K0), mx_kscale(K1), mx_kscale(K2)
    r = np.exp2(np.random.uniform(-2.0, 2.0, (B, 1))) / (KT * PT) ** 0.25
    return {"target_grad": bf(np.random.standard_normal((B, PT)) * r),
            "embedding": bf(np.random.standard_normal((B, KT)) * r * np.concatenate([t0, t1, t2])),
            "bases0": bf(np.random.standard_normal((P0, K0)) / np.sqrt(P0) / t0[None, :]),
            "bases1": bf(np.random.standard_normal((P1, K1)) / np.sqrt(P1) / t1[None, :]),
            "bases2": bf(np.random.standard_normal((P2, K2)) / np.sqrt(P2) / t2[None, :])}


def reference(target_grad, embedding, bases0, bases1, bases2):
    g = f64(target_grad)
    e = f64(embedding)
    approx_parts = []
    offset = 0
    for b in (f64(bases0), f64(bases1), f64(bases2)):
        num_k = b.shape[1]
        approx_parts.append(mxq(e[:, offset:offset + num_k], 1, "e4m3") @ mxq(b.T, 0, "e4m3"))
        offset += num_k
    no_reduction_approx = np.concatenate(approx_parts, axis=1)
    residual = g - no_reduction_approx
    return np.sum(clip_rows(residual, CLIP1), axis=0) / B

@@ -1,0 +1,218 @@
+from contextlib import ExitStack
+
+import concourse.mybir as mybir
+from concourse.masks import make_identity
+
+F32 = mybir.dt.float32
+BF16 = mybir.dt.bfloat16
+U32 = mybir.dt.uint32
+U8 = mybir.dt.uint8
+FP8X4 = mybir.dt.float8_e4m3fn_x4
+ALU = mybir.AluOpType
+ACT = mybir.ActivationFunctionType
+AXIS = mybir.AxisListType
+
+P = 128
+BATCH = 4096
+GROUPS = 3
+K_GROUP = 512
+K_ALL = GROUPS * K_GROUP
+J_ALL = GROUPS * P
+TILES = BATCH // P
+STEP_TILES = 2
+STEPS = TILES // STEP_TILES
+STEP_UNITS = STEP_TILES * GROUPS
+UNIT_WORDS = K_GROUP // 2
+BANK_UNITS = 2
+STEP_BANKS = STEP_UNITS // BANK_UNITS
+GRAD_LOAD_STEPS = 4
+QUANTISE_LAG = 1
+MULTIPLY_LAG = 2
+SQUARE_LAG = 3
+SCALE_LAG = 4
+ADD_LAG = 5
+VECTOR_COPY_EVERY = 4
+
+FLOPS = 2 * BATCH * K_ALL * P
+
+
+def tile_gep_pb_t_kernel(tc, target_grad, embedding, bases0, bases1, bases2, out):
+    nc = tc.nc
+    with ExitStack() as ctx:
+        ctx.enter_context(tc.manual_schedule())
+        const = ctx.enter_context(tc.tile_pool(name="const", bufs=1))
+        e_pool = ctx.enter_context(tc.tile_pool(name="e_pool", bufs=STEPS))
+        g_pool = ctx.enter_context(tc.tile_pool(name="g_pool", bufs=STEPS // GRAD_LOAD_STEPS))
+        grouped_pool = ctx.enter_context(tc.tile_pool(name="grouped_pool", bufs=3))
+        mx_pool = ctx.enter_context(tc.tile_pool(name="mx_pool", bufs=3))
+        resid_pool = ctx.enter_context(tc.tile_pool(name="resid_pool", bufs=ADD_LAG - MULTIPLY_LAG + 3))
+        small_pool = ctx.enter_context(tc.tile_pool(name="small_pool", bufs=5))
+        flip_psum = ctx.enter_context(tc.psum_pool(name="flip_psum", bufs=4))
+        approx_psum = ctx.enter_context(tc.psum_pool(name="approx_psum", bufs=3))
+        sums_psum = ctx.enter_context(tc.psum_pool(name="sums_psum", bufs=1))
+
+        emb_rows = embedding.rearrange("(p t) k -> p (t k)", t=TILES)
+        grad_rows = target_grad.rearrange("(p t) j -> p (t j)", t=TILES)
+        b_raw = const.tile([P, K_ALL], BF16)
+        for g, bases in enumerate((bases0, bases1, bases2)):
+            nc.scalar.dma_start(out=b_raw[:, g * K_GROUP : (g + 1) * K_GROUP], in_=bases)
+        e_raw = []
+        g_raw = []
+        for s in range(STEPS):
+            e_step = e_pool.tile([P, STEP_TILES * K_ALL], BF16)
+            nc.sync.dma_start(out=e_step[:], in_=emb_rows[:, s * STEP_TILES * K_ALL : (s + 1) * STEP_TILES * K_ALL])
+            e_raw.append(e_step)
+            if s % GRAD_LOAD_STEPS == 1:
+                g_cols = GRAD_LOAD_STEPS * STEP_TILES * J_ALL
+                g_load = g_pool.tile([P, g_cols], BF16)
+                nc.sync.dma_start(out=g_load[:], in_=grad_rows[:, len(g_raw) * g_cols : (len(g_raw) + 1) * g_cols])
+                g_raw.append(g_load)
+
+        ident = const.tile([P, P], F32)
+        make_identity(nc, ident[:])
+        totals = const.tile([P, P], F32)
+        nc.vector.memset(totals[:], 0.0)
+        warm = const.tile([P, 1], F32)
+        nc.vector.memset(warm[:], 1.0)
+        nc.scalar.activation(out=warm[:], in_=warm[:], func=ACT.Abs_reciprocal_sqrt)
+
+        def flip_units(src, grouped, first_unit, n_units, on_vector):
+            src_words = src[:].bitcast(F32)
+            grouped_words = grouped[:].bitcast(F32)
+            flipped = flip_psum.tile([P, BANK_UNITS, 2, P], F32)
+            for n in range(n_units):
+                for h in range(2):
+                    unit_words = src_words[:, (first_unit + n) * UNIT_WORDS : (first_unit + n + 1) * UNIT_WORDS]
+                    nc.tensor.transpose(flipped[:, n, h, :], unit_words[:, h : UNIT_WORDS : 2], ident[:])
+            dst = grouped_words[:, first_unit * UNIT_WORDS : (first_unit + n_units) * UNIT_WORDS]
+            dst = dst.rearrange("p (n r h) -> p n r h", n=n_units, h=2)
+            flipped_rows = flipped[:, 0:n_units, :, :].rearrange("p n h r -> p n r h")
+            if on_vector:
+                nc.vector.tensor_copy(out=dst, in_=flipped_rows)
+            else:
+                nc.scalar.copy(out=dst, in_=flipped_rows)
+
+        def quantise_units(grouped, codes, scales, first_unit, n_units):
+            cols = slice(first_unit * P, (first_unit + n_units) * P)
+            nc.vector.quantize_mx(
+                out=codes[:, cols].bitcast(FP8X4),
+                scales=scales[:, cols],
+                in_=grouped[:, first_unit * K_GROUP : (first_unit + n_units) * K_GROUP],
+            )
+
+        b_grouped = const.tile([P, K_ALL], BF16, align_bytes=64)
+        b_codes = const.tile([P, J_ALL], U32, align_bytes=64)
+        b_scales = const.tile([P, J_ALL], U8, align_bytes=64)
+        for g in range(GROUPS):
+            flip_units(b_raw, b_grouped, g, 1, False)
+        for g in range(GROUPS):
+            quantise_units(b_grouped, b_codes, b_scales, g, 1)
+
+        grouped_of = {}
+        codes_of = {}
+        scales_of = {}
+        resid_of = {}
+        sumsq_of = {}
+        factor_of = {}
+        flipped_sums = sums_psum.tile([P, GROUPS, P], F32)
+
+        def flip(s):
+            grouped = grouped_pool.tile([P, STEP_UNITS * K_GROUP], BF16, align_bytes=64)
+            grouped_of[s] = grouped
+            for bank in range(STEP_BANKS):
+                on_vector = (s * STEP_BANKS + bank) % VECTOR_COPY_EVERY == VECTOR_COPY_EVERY - 1
+                flip_units(e_raw[s], grouped, bank * BANK_UNITS, BANK_UNITS, on_vector)
+
+        def quantise(s):
+            codes = mx_pool.tile([P, STEP_UNITS * P], U32, align_bytes=64)
+            scales = mx_pool.tile([P, STEP_UNITS * P], U8, align_bytes=64)
+            codes_of[s] = codes
+            scales_of[s] = scales
+            for bank in range(STEP_BANKS):
+                quantise_units(grouped_of[s], codes, scales, bank * BANK_UNITS, BANK_UNITS)
+
+        def multiply(s):
+            resid = resid_pool.tile([P, STEP_TILES * J_ALL], F32)
+            resid_of[s] = resid
+            for t in range(STEP_TILES):
+                approx = approx_psum.tile([P, J_ALL], F32)
+                for g in range(GROUPS):
+                    unit_cols = slice((t * GROUPS + g) * P, (t * GROUPS + g + 1) * P)
+                    g_cols = slice(g * P, (g + 1) * P)
+                    nc.tensor.matmul_mx(
+                        out=approx[:, g_cols],
+                        lhsT=codes_of[s][:, unit_cols].bitcast(FP8X4),
+                        lhsT_scale=scales_of[s][:, unit_cols],
+                        rhs=b_codes[:, g_cols].bitcast(FP8X4),
+                        rhs_scale=b_scales[:, g_cols],
+                        start=True,
+                        stop=True,
+                    )
+                grad_first = ((s % GRAD_LOAD_STEPS) * STEP_TILES + t) * J_ALL
+                nc.vector.tensor_tensor(
+                    out=resid[:, t * J_ALL : (t + 1) * J_ALL],
+                    in0=g_raw[s // GRAD_LOAD_STEPS][:, grad_first : grad_first + J_ALL],
+                    in1=approx[:],
+                    op=ALU.subtract,
+                )
+
+        def square(s):
+            sumsq = small_pool.tile([P, STEP_TILES], F32)
+            sumsq_of[s] = sumsq
+            for t in range(STEP_TILES):
+                squares = small_pool.tile([P, J_ALL], BF16)
+                nc.scalar.activation(
+                    out=squares[:],
+                    in_=resid_of[s][:, t * J_ALL : (t + 1) * J_ALL],
+                    func=ACT.Square,
+                    accum_out=sumsq[:, t : t + 1],
+                )
+
+        def clip_factor(s):
+            excess = small_pool.tile([P, STEP_TILES], F32)
+            nc.scalar.activation(out=excess[:], in_=sumsq_of[s][:], func=ACT.Relu, bias=-1.0)
+            factor = small_pool.tile([P, STEP_TILES], F32)
+            nc.scalar.activation(out=factor[:], in_=excess[:], func=ACT.Abs_reciprocal_sqrt, bias=1.0)
+            factor_of[s] = factor
+
+        def scale(s):
+            for t in range(STEP_TILES):
+                resid_t = resid_of[s][:, t * J_ALL : (t + 1) * J_ALL]
+                nc.gpsimd.tensor_scalar(
+                    out=resid_t, in0=resid_t, scalar1=factor_of[s][:, t : t + 1], scalar2=0.0, op0=ALU.mult, op1=ALU.add
+                )
+
+        def add_up(s):
+            for t in range(STEP_TILES):
+                for g in range(GROUPS):
+                    unit_cols = slice((t * GROUPS + g) * P, (t * GROUPS + g + 1) * P)
+                    nc.tensor.matmul(
+                        out=flipped_sums[:, g, :],
+                        lhsT=resid_of[s][:, unit_cols],
+                        rhs=ident[:],
+                        is_transpose=True,
+                        start=(s == 0 and t == 0 and g == 0),
+                        stop=(s == STEPS - 1 and t == STEP_TILES - 1 and g == GROUPS - 1),
+                    )
+
+        for turn in range(STEPS + ADD_LAG):
+            if 0 <= turn - QUANTISE_LAG < STEPS:
+                quantise(turn - QUANTISE_LAG)
+            if turn < STEPS:
+                flip(turn)
+            if 0 <= turn - MULTIPLY_LAG < STEPS:
+                multiply(turn - MULTIPLY_LAG)
+            if 0 <= turn - SQUARE_LAG < STEPS:
+                square(turn - SQUARE_LAG)
+                clip_factor(turn - SQUARE_LAG)
+            if 0 <= turn - SCALE_LAG < STEPS:
+                scale(turn - SCALE_LAG)
+            if 0 <= turn - ADD_LAG < STEPS:
+                add_up(turn - ADD_LAG)
+
+        nc.vector.tensor_reduce(out=totals[:, 0:GROUPS], in_=flipped_sums[:], axis=AXIS.X, op=ALU.add)
+        totals_flipped = flip_psum.tile([P, P], F32, tag="flipped")
+        nc.tensor.transpose(totals_flipped[:], totals[:], ident[:])
+        mean = const.tile([P, P], F32)
+        nc.scalar.mul(out=mean[:], in_=totals_flipped[:], mul=1.0 / BATCH)
+        nc.sync.dma_start(out=out.rearrange("(g j) -> g j", g=GROUPS), in_=mean[0:GROUPS, :])

@@ -31,7 +31,6 @@ MULTIPLY_LAG = 2
 SQUARE_LAG = 3
 SCALE_LAG = 4
 ADD_LAG = 5
-VECTOR_COPY_EVERY = 4
 
 FLOPS = 2 * BATCH * K_ALL * P
 
@@ -54,14 +53,19 @@ def tile_gep_pb_t_kernel(tc, target_grad, embedding, bases0, bases1, bases2, out
         emb_rows = embedding.rearrange("(p t) k -> p (t k)", t=TILES)
         grad_rows = target_grad.rearrange("(p t) j -> p (t j)", t=TILES)
         b_raw = const.tile([P, K_ALL], BF16)
-        for g, bases in enumerate((bases0, bases1, bases2)):
-            nc.scalar.dma_start(out=b_raw[:, g * K_GROUP : (g + 1) * K_GROUP], in_=bases)
         e_raw = []
         g_raw = []
         for s in range(STEPS):
             e_step = e_pool.tile([P, STEP_TILES * K_ALL], BF16)
-            nc.sync.dma_start(out=e_step[:], in_=emb_rows[:, s * STEP_TILES * K_ALL : (s + 1) * STEP_TILES * K_ALL])
+            pieces = STEP_TILES if s == 0 else 1
+            piece = STEP_TILES * K_ALL // pieces
+            for i in range(pieces):
+                first = s * STEP_TILES * K_ALL + i * piece
+                nc.sync.dma_start(out=e_step[:, i * piece : (i + 1) * piece], in_=emb_rows[:, first : first + piece])
             e_raw.append(e_step)
+            if s == 0:
+                for g, bases in enumerate((bases0, bases1, bases2)):
+                    nc.sync.dma_start(out=b_raw[:, g * K_GROUP : (g + 1) * K_GROUP], in_=bases)
             if s % GRAD_LOAD_STEPS == 1:
                 g_cols = GRAD_LOAD_STEPS * STEP_TILES * J_ALL
                 g_load = g_pool.tile([P, g_cols], BF16)
@@ -103,33 +107,29 @@ def tile_gep_pb_t_kernel(tc, target_grad, embedding, bases0, bases1, bases2, out
         b_grouped = const.tile([P, K_ALL], BF16, align_bytes=64)
         b_codes = const.tile([P, J_ALL], U32, align_bytes=64)
         b_scales = const.tile([P, J_ALL], U8, align_bytes=64)
-        for g in range(GROUPS):
-            flip_units(b_raw, b_grouped, g, 1, False)
-        for g in range(GROUPS):
-            quantise_units(b_grouped, b_codes, b_scales, g, 1)
 
         grouped_of = {}
         codes_of = {}
         scales_of = {}
         resid_of = {}
         sumsq_of = {}
+        excess_of = {}
         factor_of = {}
-        flipped_sums = sums_psum.tile([P, GROUPS, P], F32)
 
-        def flip(s):
-            grouped = grouped_pool.tile([P, STEP_UNITS * K_GROUP], BF16, align_bytes=64)
-            grouped_of[s] = grouped
-            for bank in range(STEP_BANKS):
-                on_vector = (s * STEP_BANKS + bank) % VECTOR_COPY_EVERY == VECTOR_COPY_EVERY - 1
-                flip_units(e_raw[s], grouped, bank * BANK_UNITS, BANK_UNITS, on_vector)
+        def flip_bank(s, bank):
+            if bank == 0:
+                grouped = grouped_pool.tile([P, STEP_UNITS * K_GROUP], BF16, align_bytes=64)
+                grouped_of[s] = grouped
+            on_vector = bank == 0 and s % 4 != 3 or bank == 2 and s == 0
+            flip_units(e_raw[s], grouped_of[s], bank * BANK_UNITS, BANK_UNITS, on_vector)
 
-        def quantise(s):
-            codes = mx_pool.tile([P, STEP_UNITS * P], U32, align_bytes=64)
-            scales = mx_pool.tile([P, STEP_UNITS * P], U8, align_bytes=64)
-            codes_of[s] = codes
-            scales_of[s] = scales
-            for bank in range(STEP_BANKS):
-                quantise_units(grouped_of[s], codes, scales, bank * BANK_UNITS, BANK_UNITS)
+        def quantise(s, first_unit, n_units):
+            if first_unit == 0:
+                codes = mx_pool.tile([P, STEP_UNITS * P], U32, align_bytes=64)
+                scales = mx_pool.tile([P, STEP_UNITS * P], U8, align_bytes=64)
+                codes_of[s] = codes
+                scales_of[s] = scales
+            quantise_units(grouped_of[s], codes_of[s], scales_of[s], first_unit, n_units)
 
         def multiply(s):
             resid = resid_pool.tile([P, STEP_TILES * J_ALL], F32)
@@ -156,31 +156,38 @@ def tile_gep_pb_t_kernel(tc, target_grad, embedding, bases0, bases1, bases2, out
                     op=ALU.subtract,
                 )
 
-        def square(s):
-            sumsq = small_pool.tile([P, STEP_TILES], F32)
-            sumsq_of[s] = sumsq
-            for t in range(STEP_TILES):
-                squares = small_pool.tile([P, J_ALL], BF16)
-                nc.scalar.activation(
-                    out=squares[:],
-                    in_=resid_of[s][:, t * J_ALL : (t + 1) * J_ALL],
-                    func=ACT.Square,
-                    accum_out=sumsq[:, t : t + 1],
-                )
+        def square(s, t):
+            if t == 0:
+                sumsq = small_pool.tile([P, STEP_TILES], F32)
+                sumsq_of[s] = sumsq
+            squares = small_pool.tile([P, J_ALL], BF16)
+            nc.scalar.activation(
+                out=squares[:],
+                in_=resid_of[s][:, t * J_ALL : (t + 1) * J_ALL],
+                func=ACT.Square,
+                accum_out=sumsq_of[s][:, t : t + 1],
+            )
 
-        def clip_factor(s):
+        def clip_excess(s):
             excess = small_pool.tile([P, STEP_TILES], F32)
             nc.scalar.activation(out=excess[:], in_=sumsq_of[s][:], func=ACT.Relu, bias=-1.0)
+            excess_of[s] = excess
+
+        def clip_factor(s):
             factor = small_pool.tile([P, STEP_TILES], F32)
-            nc.scalar.activation(out=factor[:], in_=excess[:], func=ACT.Abs_reciprocal_sqrt, bias=1.0)
+            nc.scalar.activation(out=factor[:], in_=excess_of[s][:], func=ACT.Abs_reciprocal_sqrt, bias=1.0)
             factor_of[s] = factor
 
         def scale(s):
             for t in range(STEP_TILES):
                 resid_t = resid_of[s][:, t * J_ALL : (t + 1) * J_ALL]
-                nc.gpsimd.tensor_scalar(
-                    out=resid_t, in0=resid_t, scalar1=factor_of[s][:, t : t + 1], scalar2=0.0, op0=ALU.mult, op1=ALU.add
-                )
+                factor_t = factor_of[s][:, t : t + 1]
+                if s == STEPS - 1 and t == STEP_TILES - 1:
+                    nc.vector.tensor_scalar(out=resid_t, in0=resid_t, scalar1=factor_t, scalar2=0.0, op0=ALU.mult, op1=ALU.add)
+                else:
+                    nc.gpsimd.tensor_scalar(out=resid_t, in0=resid_t, scalar1=factor_t, scalar2=0.0, op0=ALU.mult, op1=ALU.add)
+
+        flipped_sums = sums_psum.tile([P, GROUPS, P], F32)
 
         def add_up(s):
             for t in range(STEP_TILES):
@@ -196,19 +203,35 @@ def tile_gep_pb_t_kernel(tc, target_grad, embedding, bases0, bases1, bases2, out
                     )
 
         for turn in range(STEPS + ADD_LAG):
-            if 0 <= turn - QUANTISE_LAG < STEPS:
-                quantise(turn - QUANTISE_LAG)
+            to_multiply = turn - MULTIPLY_LAG
+            to_quantise = turn - QUANTISE_LAG
+            to_square = turn - SQUARE_LAG
+            to_scale = turn - SCALE_LAG
+            to_add = turn - ADD_LAG
+            if 0 <= to_multiply < STEPS:
+                multiply(to_multiply)
+            if 0 <= to_quantise < STEPS:
+                quantise(to_quantise, 0, BANK_UNITS)
+                quantise(to_quantise, BANK_UNITS, STEP_UNITS - BANK_UNITS)
+            if 0 <= to_scale < STEPS:
+                clip_excess(to_scale)
+            if 0 <= to_square < STEPS:
+                square(to_square, 0)
+            if 0 <= to_scale < STEPS:
+                clip_factor(to_scale)
+                scale(to_scale)
+            if 0 <= to_square < STEPS:
+                square(to_square, 1)
             if turn < STEPS:
-                flip(turn)
-            if 0 <= turn - MULTIPLY_LAG < STEPS:
-                multiply(turn - MULTIPLY_LAG)
-            if 0 <= turn - SQUARE_LAG < STEPS:
-                square(turn - SQUARE_LAG)
-                clip_factor(turn - SQUARE_LAG)
-            if 0 <= turn - SCALE_LAG < STEPS:
-                scale(turn - SCALE_LAG)
-            if 0 <= turn - ADD_LAG < STEPS:
-                add_up(turn - ADD_LAG)
+                for bank in range(STEP_BANKS):
+                    flip_bank(turn, bank)
+            if 0 <= to_add < STEPS:
+                add_up(to_add)
+            if turn == 0:
+                flip_units(b_raw, b_grouped, 0, 2, False)
+                flip_units(b_raw, b_grouped, 2, 1, True)
+                quantise_units(b_grouped, b_codes, b_scales, 0, 2)
+                quantise_units(b_grouped, b_codes, b_scales, 2, 1)
 
         nc.vector.tensor_reduce(out=totals[:, 0:GROUPS], in_=flipped_sums[:], axis=AXIS.X, op=ALU.add)
         totals_flipped = flip_psum.tile([P, P], F32, tag="flipped")

@@ -21,11 +21,15 @@ J_ALL = GROUPS * P
 TILES = BATCH // P
 STEP_TILES = 2
 STEPS = TILES // STEP_TILES
+LAST = STEPS - 1
 STEP_UNITS = STEP_TILES * GROUPS
 UNIT_WORDS = K_GROUP // 2
 BANK_UNITS = 2
 STEP_BANKS = STEP_UNITS // BANK_UNITS
-GRAD_LOAD_STEPS = 4
+GRAD_FIRST_STEPS = (0, 2, 4, 8, 12)
+VECTOR_COPY_STEPS = (0, 1)
+SORTED_BANK = 2
+FIRST_SORTED_STEP = 3
 QUANTISE_LAG = 1
 MULTIPLY_LAG = 2
 SQUARE_LAG = 3
@@ -41,7 +45,8 @@ def tile_gep_pb_t_kernel(tc, target_grad, embedding, bases0, bases1, bases2, out
         ctx.enter_context(tc.manual_schedule())
         const = ctx.enter_context(tc.tile_pool(name="const", bufs=1))
         e_pool = ctx.enter_context(tc.tile_pool(name="e_pool", bufs=STEPS))
-        g_pool = ctx.enter_context(tc.tile_pool(name="g_pool", bufs=STEPS // GRAD_LOAD_STEPS))
+        g_pool = ctx.enter_context(tc.tile_pool(name="g_pool", bufs=len(GRAD_FIRST_STEPS)))
+        sorted_pool = ctx.enter_context(tc.tile_pool(name="sorted_pool", bufs=3))
         grouped_pool = ctx.enter_context(tc.tile_pool(name="grouped_pool", bufs=3))
         mx_pool = ctx.enter_context(tc.tile_pool(name="mx_pool", bufs=3))
         resid_pool = ctx.enter_context(tc.tile_pool(name="resid_pool", bufs=ADD_LAG - MULTIPLY_LAG + 3))
@@ -54,10 +59,10 @@ def tile_gep_pb_t_kernel(tc, target_grad, embedding, bases0, bases1, bases2, out
         grad_rows = target_grad.rearrange("(p t) j -> p (t j)", t=TILES)
         b_raw = const.tile([P, K_ALL], BF16)
         e_raw = []
-        g_raw = []
+        g_raw = {}
         for s in range(STEPS):
             e_step = e_pool.tile([P, STEP_TILES * K_ALL], BF16)
-            pieces = STEP_TILES if s == 0 else 1
+            pieces = STEP_BANKS if s == 0 else 1
             piece = STEP_TILES * K_ALL // pieces
             for i in range(pieces):
                 first = s * STEP_TILES * K_ALL + i * piece
@@ -66,11 +71,14 @@ def tile_gep_pb_t_kernel(tc, target_grad, embedding, bases0, bases1, bases2, out
             if s == 0:
                 for g, bases in enumerate((bases0, bases1, bases2)):
                     nc.sync.dma_start(out=b_raw[:, g * K_GROUP : (g + 1) * K_GROUP], in_=bases)
-            if s % GRAD_LOAD_STEPS == 1:
-                g_cols = GRAD_LOAD_STEPS * STEP_TILES * J_ALL
-                g_load = g_pool.tile([P, g_cols], BF16)
-                nc.sync.dma_start(out=g_load[:], in_=grad_rows[:, len(g_raw) * g_cols : (len(g_raw) + 1) * g_cols])
-                g_raw.append(g_load)
+            if s - 1 in GRAD_FIRST_STEPS:
+                load = GRAD_FIRST_STEPS.index(s - 1)
+                end = GRAD_FIRST_STEPS[load + 1] if load + 1 < len(GRAD_FIRST_STEPS) else STEPS
+                step_cols = STEP_TILES * J_ALL
+                g_load = g_pool.tile([P, (end - s + 1) * step_cols], BF16)
+                nc.sync.dma_start(out=g_load[:], in_=grad_rows[:, (s - 1) * step_cols : end * step_cols])
+                for i in range(s - 1, end):
+                    g_raw[i] = (g_load, (i - s + 1) * step_cols)
 
         ident = const.tile([P, P], F32)
         make_identity(nc, ident[:])
@@ -80,14 +88,18 @@ def tile_gep_pb_t_kernel(tc, target_grad, embedding, bases0, bases1, bases2, out
         nc.vector.memset(warm[:], 1.0)
         nc.scalar.activation(out=warm[:], in_=warm[:], func=ACT.Abs_reciprocal_sqrt)
 
-        def flip_units(src, grouped, first_unit, n_units, on_vector):
+        def flip_units(src, grouped, first_unit, n_units, on_vector, sorted_words=None):
             src_words = src[:].bitcast(F32)
             grouped_words = grouped[:].bitcast(F32)
             flipped = flip_psum.tile([P, BANK_UNITS, 2, P], F32)
             for n in range(n_units):
                 for h in range(2):
-                    unit_words = src_words[:, (first_unit + n) * UNIT_WORDS : (first_unit + n + 1) * UNIT_WORDS]
-                    nc.tensor.transpose(flipped[:, n, h, :], unit_words[:, h : UNIT_WORDS : 2], ident[:])
+                    if sorted_words is None:
+                        unit_words = src_words[:, (first_unit + n) * UNIT_WORDS : (first_unit + n + 1) * UNIT_WORDS]
+                        half = unit_words[:, h : UNIT_WORDS : 2]
+                    else:
+                        half = sorted_words[:, (2 * n + h) * P : (2 * n + h + 1) * P]
+                    nc.tensor.transpose(flipped[:, n, h, :], half, ident[:])
             dst = grouped_words[:, first_unit * UNIT_WORDS : (first_unit + n_units) * UNIT_WORDS]
             dst = dst.rearrange("p (n r h) -> p n r h", n=n_units, h=2)
             flipped_rows = flipped[:, 0:n_units, :, :].rearrange("p n h r -> p n r h")
@@ -108,6 +120,7 @@ def tile_gep_pb_t_kernel(tc, target_grad, embedding, bases0, bases1, bases2, out
         b_codes = const.tile([P, J_ALL], U32, align_bytes=64)
         b_scales = const.tile([P, J_ALL], U8, align_bytes=64)
 
+        sorted_of = {}
         grouped_of = {}
         codes_of = {}
         scales_of = {}
@@ -120,8 +133,19 @@ def tile_gep_pb_t_kernel(tc, target_grad, embedding, bases0, bases1, bases2, out
             if bank == 0:
                 grouped = grouped_pool.tile([P, STEP_UNITS * K_GROUP], BF16, align_bytes=64)
                 grouped_of[s] = grouped
-            on_vector = bank == 0 and s % 4 != 3 or bank == 2 and s == 0
-            flip_units(e_raw[s], grouped_of[s], bank * BANK_UNITS, BANK_UNITS, on_vector)
+            on_vector = bank == 0 and s % 3 in VECTOR_COPY_STEPS or bank == 2 and s == 0 or bank == 1 and s == LAST
+            sorted_words = sorted_of[s] if bank == SORTED_BANK and s in sorted_of else None
+            flip_units(e_raw[s], grouped_of[s], bank * BANK_UNITS, BANK_UNITS, on_vector, sorted_words)
+
+        def sort_bank(s):
+            words = sorted_pool.tile([P, BANK_UNITS * UNIT_WORDS], F32)
+            first_word = SORTED_BANK * BANK_UNITS * UNIT_WORDS
+            src = e_raw[s][:].bitcast(F32)[:, first_word : first_word + BANK_UNITS * UNIT_WORDS]
+            nc.vector.tensor_copy(
+                out=words[:].rearrange("p (n h w) -> p n h w", n=BANK_UNITS, h=2),
+                in_=src.rearrange("p (n w h) -> p n h w", n=BANK_UNITS, h=2),
+            )
+            sorted_of[s] = words
 
         def quantise(s, first_unit, n_units):
             if first_unit == 0:
@@ -148,10 +172,10 @@ def tile_gep_pb_t_kernel(tc, target_grad, embedding, bases0, bases1, bases2, out
                         start=True,
                         stop=True,
                     )
-                grad_first = ((s % GRAD_LOAD_STEPS) * STEP_TILES + t) * J_ALL
+                g_load, g_first = g_raw[s]
                 nc.vector.tensor_tensor(
                     out=resid[:, t * J_ALL : (t + 1) * J_ALL],
-                    in0=g_raw[s // GRAD_LOAD_STEPS][:, grad_first : grad_first + J_ALL],
+                    in0=g_load[:, g_first + t * J_ALL : g_first + (t + 1) * J_ALL],
                     in1=approx[:],
                     op=ALU.subtract,
                 )
@@ -160,13 +184,20 @@ def tile_gep_pb_t_kernel(tc, target_grad, embedding, bases0, bases1, bases2, out
             if t == 0:
                 sumsq = small_pool.tile([P, STEP_TILES], F32)
                 sumsq_of[s] = sumsq
+            resid_t = resid_of[s][:, t * J_ALL : (t + 1) * J_ALL]
             squares = small_pool.tile([P, J_ALL], BF16)
-            nc.scalar.activation(
-                out=squares[:],
-                in_=resid_of[s][:, t * J_ALL : (t + 1) * J_ALL],
-                func=ACT.Square,
-                accum_out=sumsq_of[s][:, t : t + 1],
-            )
+            if s == LAST and t == STEP_TILES - 1:
+                nc.vector.scalar_tensor_tensor(
+                    out=squares[:],
+                    in0=resid_t,
+                    scalar=1.0,
+                    in1=resid_t,
+                    op0=ALU.mult,
+                    op1=ALU.mult,
+                    accum_out=sumsq_of[s][:, t : t + 1],
+                )
+            else:
+                nc.scalar.activation(out=squares[:], in_=resid_t, func=ACT.Square, accum_out=sumsq_of[s][:, t : t + 1])
 
         def clip_excess(s):
             excess = small_pool.tile([P, STEP_TILES], F32)
@@ -181,11 +212,15 @@ def tile_gep_pb_t_kernel(tc, target_grad, embedding, bases0, bases1, bases2, out
         def scale(s):
             for t in range(STEP_TILES):
                 resid_t = resid_of[s][:, t * J_ALL : (t + 1) * J_ALL]
-                factor_t = factor_of[s][:, t : t + 1]
-                if s == STEPS - 1 and t == STEP_TILES - 1:
-                    nc.vector.tensor_scalar(out=resid_t, in0=resid_t, scalar1=factor_t, scalar2=0.0, op0=ALU.mult, op1=ALU.add)
-                else:
-                    nc.gpsimd.tensor_scalar(out=resid_t, in0=resid_t, scalar1=factor_t, scalar2=0.0, op0=ALU.mult, op1=ALU.add)
+                engine = nc.vector if s >= LAST - 1 and t == STEP_TILES - 1 else nc.gpsimd
+                engine.tensor_scalar(
+                    out=resid_t,
+                    in0=resid_t,
+                    scalar1=factor_of[s][:, t : t + 1],
+                    scalar2=0.0,
+                    op0=ALU.mult,
+                    op1=ALU.add,
+                )
 
         flipped_sums = sums_psum.tile([P, GROUPS, P], F32)
 
@@ -199,7 +234,7 @@ def tile_gep_pb_t_kernel(tc, target_grad, embedding, bases0, bases1, bases2, out
                         rhs=ident[:],
                         is_transpose=True,
                         start=(s == 0 and t == 0 and g == 0),
-                        stop=(s == STEPS - 1 and t == STEP_TILES - 1 and g == GROUPS - 1),
+                        stop=(s == LAST and t == STEP_TILES - 1 and g == GROUPS - 1),
                     )
 
         for turn in range(STEPS + ADD_LAG):
@@ -210,21 +245,24 @@ def tile_gep_pb_t_kernel(tc, target_grad, embedding, bases0, bases1, bases2, out
             to_add = turn - ADD_LAG
             if 0 <= to_multiply < STEPS:
                 multiply(to_multiply)
-            if 0 <= to_quantise < STEPS:
-                quantise(to_quantise, 0, BANK_UNITS)
-                quantise(to_quantise, BANK_UNITS, STEP_UNITS - BANK_UNITS)
             if 0 <= to_scale < STEPS:
                 clip_excess(to_scale)
             if 0 <= to_square < STEPS:
                 square(to_square, 0)
             if 0 <= to_scale < STEPS:
                 clip_factor(to_scale)
-                scale(to_scale)
             if 0 <= to_square < STEPS:
                 square(to_square, 1)
+            if 0 <= to_scale < STEPS:
+                scale(to_scale)
+            if 0 <= to_quantise < STEPS:
+                quantise(to_quantise, 0, BANK_UNITS)
+                quantise(to_quantise, BANK_UNITS, STEP_UNITS - BANK_UNITS)
             if turn < STEPS:
                 for bank in range(STEP_BANKS):
                     flip_bank(turn, bank)
+            if FIRST_SORTED_STEP <= turn + 1 < STEPS:
+                sort_bank(turn + 1)
             if 0 <= to_add < STEPS:
                 add_up(to_add)
             if turn == 0:

@@ -27,7 +27,8 @@ UNIT_WORDS = K_GROUP // 2
 BANK_UNITS = 2
 STEP_BANKS = STEP_UNITS // BANK_UNITS
 GRAD_FIRST_STEPS = (0, 2, 4, 8, 12)
-VECTOR_COPY_STEPS = (0, 1)
+VECTOR_COPY_EVERY = 2
+DRAIN_STEPS = 3
 SORTED_BANK = 2
 FIRST_SORTED_STEP = 3
 QUANTISE_LAG = 1
@@ -133,7 +134,7 @@ def tile_gep_pb_t_kernel(tc, target_grad, embedding, bases0, bases1, bases2, out
             if bank == 0:
                 grouped = grouped_pool.tile([P, STEP_UNITS * K_GROUP], BF16, align_bytes=64)
                 grouped_of[s] = grouped
-            on_vector = bank == 0 and s % 3 in VECTOR_COPY_STEPS or bank == 2 and s == 0 or bank == 1 and s == LAST
+            on_vector = bank == 0 and s % VECTOR_COPY_EVERY == 0 or bank == 2 and s == 0 or bank == 1 and s == LAST
             sorted_words = sorted_of[s] if bank == SORTED_BANK and s in sorted_of else None
             flip_units(e_raw[s], grouped_of[s], bank * BANK_UNITS, BANK_UNITS, on_vector, sorted_words)
 
@@ -212,7 +213,7 @@ def tile_gep_pb_t_kernel(tc, target_grad, embedding, bases0, bases1, bases2, out
         def scale(s):
             for t in range(STEP_TILES):
                 resid_t = resid_of[s][:, t * J_ALL : (t + 1) * J_ALL]
-                engine = nc.vector if s >= LAST - 1 and t == STEP_TILES - 1 else nc.gpsimd
+                engine = nc.vector if s >= STEPS - DRAIN_STEPS else nc.gpsimd
                 engine.tensor_scalar(
                     out=resid_t,
                     in0=resid_t,
@@ -243,6 +244,9 @@ def tile_gep_pb_t_kernel(tc, target_grad, embedding, bases0, bases1, bases2, out
             to_square = turn - SQUARE_LAG
             to_scale = turn - SCALE_LAG
             to_add = turn - ADD_LAG
+            if 0 <= to_quantise < STEPS:
+                quantise(to_quantise, 0, BANK_UNITS)
+                quantise(to_quantise, BANK_UNITS, STEP_UNITS - BANK_UNITS)
             if 0 <= to_multiply < STEPS:
                 multiply(to_multiply)
             if 0 <= to_scale < STEPS:
@@ -255,9 +259,6 @@ def tile_gep_pb_t_kernel(tc, target_grad, embedding, bases0, bases1, bases2, out
                 square(to_square, 1)
             if 0 <= to_scale < STEPS:
                 scale(to_scale)
-            if 0 <= to_quantise < STEPS:
-                quantise(to_quantise, 0, BANK_UNITS)
-                quantise(to_quantise, BANK_UNITS, STEP_UNITS - BANK_UNITS)
             if turn < STEPS:
                 for bank in range(STEP_BANKS):
                     flip_bank(turn, bank)

@@ -23,14 +23,14 @@ STEP_TILES = 2
 STEPS = TILES // STEP_TILES
 LAST = STEPS - 1
 STEP_UNITS = STEP_TILES * GROUPS
+BLOCK = 32
 UNIT_WORDS = K_GROUP // 2
 BANK_UNITS = 2
 STEP_BANKS = STEP_UNITS // BANK_UNITS
 GRAD_FIRST_STEPS = (0, 2, 4, 8, 12)
-VECTOR_COPY_EVERY = 2
+VECTOR_COPY_BANK = 2
+VECTOR_SUM_TILE = 0
 DRAIN_STEPS = 3
-SORTED_BANK = 2
-FIRST_SORTED_STEP = 3
 QUANTISE_LAG = 1
 MULTIPLY_LAG = 2
 SQUARE_LAG = 3
@@ -47,7 +47,6 @@ def tile_gep_pb_t_kernel(tc, target_grad, embedding, bases0, bases1, bases2, out
         const = ctx.enter_context(tc.tile_pool(name="const", bufs=1))
         e_pool = ctx.enter_context(tc.tile_pool(name="e_pool", bufs=STEPS))
         g_pool = ctx.enter_context(tc.tile_pool(name="g_pool", bufs=len(GRAD_FIRST_STEPS)))
-        sorted_pool = ctx.enter_context(tc.tile_pool(name="sorted_pool", bufs=3))
         grouped_pool = ctx.enter_context(tc.tile_pool(name="grouped_pool", bufs=3))
         mx_pool = ctx.enter_context(tc.tile_pool(name="mx_pool", bufs=3))
         resid_pool = ctx.enter_context(tc.tile_pool(name="resid_pool", bufs=ADD_LAG - MULTIPLY_LAG + 3))
@@ -83,24 +82,22 @@ def tile_gep_pb_t_kernel(tc, target_grad, embedding, bases0, bases1, bases2, out
 
         ident = const.tile([P, P], F32)
         make_identity(nc, ident[:])
-        totals = const.tile([P, P], F32)
+        sums = const.tile([P, J_ALL], F32)
+        nc.vector.memset(sums[:], 0.0)
+        totals = const.tile([P, BLOCK], F32, align_bytes=64)
         nc.vector.memset(totals[:], 0.0)
         warm = const.tile([P, 1], F32)
         nc.vector.memset(warm[:], 1.0)
         nc.scalar.activation(out=warm[:], in_=warm[:], func=ACT.Abs_reciprocal_sqrt)
 
-        def flip_units(src, grouped, first_unit, n_units, on_vector, sorted_words=None):
+        def flip_units(src, grouped, first_unit, n_units, on_vector):
             src_words = src[:].bitcast(F32)
             grouped_words = grouped[:].bitcast(F32)
             flipped = flip_psum.tile([P, BANK_UNITS, 2, P], F32)
             for n in range(n_units):
                 for h in range(2):
-                    if sorted_words is None:
-                        unit_words = src_words[:, (first_unit + n) * UNIT_WORDS : (first_unit + n + 1) * UNIT_WORDS]
-                        half = unit_words[:, h : UNIT_WORDS : 2]
-                    else:
-                        half = sorted_words[:, (2 * n + h) * P : (2 * n + h + 1) * P]
-                    nc.tensor.transpose(flipped[:, n, h, :], half, ident[:])
+                    unit_words = src_words[:, (first_unit + n) * UNIT_WORDS : (first_unit + n + 1) * UNIT_WORDS]
+                    nc.tensor.transpose(flipped[:, n, h, :], unit_words[:, h : UNIT_WORDS : 2], ident[:])
             dst = grouped_words[:, first_unit * UNIT_WORDS : (first_unit + n_units) * UNIT_WORDS]
             dst = dst.rearrange("p (n r h) -> p n r h", n=n_units, h=2)
             flipped_rows = flipped[:, 0:n_units, :, :].rearrange("p n h r -> p n r h")
@@ -121,7 +118,6 @@ def tile_gep_pb_t_kernel(tc, target_grad, embedding, bases0, bases1, bases2, out
         b_codes = const.tile([P, J_ALL], U32, align_bytes=64)
         b_scales = const.tile([P, J_ALL], U8, align_bytes=64)
 
-        sorted_of = {}
         grouped_of = {}
         codes_of = {}
         scales_of = {}
@@ -134,19 +130,8 @@ def tile_gep_pb_t_kernel(tc, target_grad, embedding, bases0, bases1, bases2, out
             if bank == 0:
                 grouped = grouped_pool.tile([P, STEP_UNITS * K_GROUP], BF16, align_bytes=64)
                 grouped_of[s] = grouped
-            on_vector = bank == 0 and s % VECTOR_COPY_EVERY == 0 or bank == 2 and s == 0 or bank == 1 and s == LAST
-            sorted_words = sorted_of[s] if bank == SORTED_BANK and s in sorted_of else None
-            flip_units(e_raw[s], grouped_of[s], bank * BANK_UNITS, BANK_UNITS, on_vector, sorted_words)
-
-        def sort_bank(s):
-            words = sorted_pool.tile([P, BANK_UNITS * UNIT_WORDS], F32)
-            first_word = SORTED_BANK * BANK_UNITS * UNIT_WORDS
-            src = e_raw[s][:].bitcast(F32)[:, first_word : first_word + BANK_UNITS * UNIT_WORDS]
-            nc.vector.tensor_copy(
-                out=words[:].rearrange("p (n h w) -> p n h w", n=BANK_UNITS, h=2),
-                in_=src.rearrange("p (n w h) -> p n h w", n=BANK_UNITS, h=2),
-            )
-            sorted_of[s] = words
+            on_vector = bank == VECTOR_COPY_BANK and s % 2 == 0
+            flip_units(e_raw[s], grouped_of[s], bank * BANK_UNITS, BANK_UNITS, on_vector)
 
         def quantise(s, first_unit, n_units):
             if first_unit == 0:
@@ -187,18 +172,7 @@ def tile_gep_pb_t_kernel(tc, target_grad, embedding, bases0, bases1, bases2, out
                 sumsq_of[s] = sumsq
             resid_t = resid_of[s][:, t * J_ALL : (t + 1) * J_ALL]
             squares = small_pool.tile([P, J_ALL], BF16)
-            if s == LAST and t == STEP_TILES - 1:
-                nc.vector.scalar_tensor_tensor(
-                    out=squares[:],
-                    in0=resid_t,
-                    scalar=1.0,
-                    in1=resid_t,
-                    op0=ALU.mult,
-                    op1=ALU.mult,
-                    accum_out=sumsq_of[s][:, t : t + 1],
-                )
-            else:
-                nc.scalar.activation(out=squares[:], in_=resid_t, func=ACT.Square, accum_out=sumsq_of[s][:, t : t + 1])
+            nc.scalar.activation(out=squares[:], in_=resid_t, func=ACT.Square, accum_out=sumsq_of[s][:, t : t + 1])
 
         def clip_excess(s):
             excess = small_pool.tile([P, STEP_TILES], F32)
@@ -207,36 +181,64 @@ def tile_gep_pb_t_kernel(tc, target_grad, embedding, bases0, bases1, bases2, out
 
         def clip_factor(s):
             factor = small_pool.tile([P, STEP_TILES], F32)
-            nc.scalar.activation(out=factor[:], in_=excess_of[s][:], func=ACT.Abs_reciprocal_sqrt, bias=1.0)
+            nc.scalar.activation(
+                out=factor[:],
+                in_=excess_of[s][:],
+                func=ACT.Abs_reciprocal_sqrt,
+                scale=float(BATCH**2),
+                bias=float(BATCH**2),
+            )
             factor_of[s] = factor
 
+        def on_vector_sum(s, t):
+            return t == VECTOR_SUM_TILE and s % 2 == 1 and s != LAST
+
         def scale(s):
+            engine = nc.vector if s >= STEPS - DRAIN_STEPS else nc.gpsimd
             for t in range(STEP_TILES):
-                resid_t = resid_of[s][:, t * J_ALL : (t + 1) * J_ALL]
-                engine = nc.vector if s >= STEPS - DRAIN_STEPS else nc.gpsimd
-                engine.tensor_scalar(
-                    out=resid_t,
-                    in0=resid_t,
-                    scalar1=factor_of[s][:, t : t + 1],
-                    scalar2=0.0,
-                    op0=ALU.mult,
-                    op1=ALU.add,
-                )
+                if not on_vector_sum(s, t):
+                    resid_t = resid_of[s][:, t * J_ALL : (t + 1) * J_ALL]
+                    engine.tensor_scalar(
+                        out=resid_t,
+                        in0=resid_t,
+                        scalar1=factor_of[s][:, t : t + 1],
+                        scalar2=0.0,
+                        op0=ALU.mult,
+                        op1=ALU.add,
+                    )
+
+        def add_on_vector(s):
+            for t in range(STEP_TILES):
+                if on_vector_sum(s, t):
+                    nc.vector.scalar_tensor_tensor(
+                        out=sums[:],
+                        in0=resid_of[s][:, t * J_ALL : (t + 1) * J_ALL],
+                        scalar=factor_of[s][:, t : t + 1],
+                        in1=sums[:],
+                        op0=ALU.mult,
+                        op1=ALU.add,
+                    )
 
         flipped_sums = sums_psum.tile([P, GROUPS, P], F32)
 
-        def add_up(s):
+        def add_flipped(src, first_col, start, stop):
+            for g in range(GROUPS):
+                nc.tensor.matmul(
+                    out=flipped_sums[:, g, :],
+                    lhsT=src[:, first_col + g * P : first_col + (g + 1) * P],
+                    rhs=ident[:],
+                    is_transpose=True,
+                    start=start and g == 0,
+                    stop=stop and g == GROUPS - 1,
+                )
+
+        def add_on_tensor(s):
+            if s == LAST:
+                add_flipped(sums, 0, False, False)
             for t in range(STEP_TILES):
-                for g in range(GROUPS):
-                    unit_cols = slice((t * GROUPS + g) * P, (t * GROUPS + g + 1) * P)
-                    nc.tensor.matmul(
-                        out=flipped_sums[:, g, :],
-                        lhsT=resid_of[s][:, unit_cols],
-                        rhs=ident[:],
-                        is_transpose=True,
-                        start=(s == 0 and t == 0 and g == 0),
-                        stop=(s == LAST and t == STEP_TILES - 1 and g == GROUPS - 1),
-                    )
+                if not on_vector_sum(s, t):
+                    tile_index = s * STEP_TILES + t
+                    add_flipped(resid_of[s], t * J_ALL, tile_index == 0, tile_index == TILES - 1)
 
         for turn in range(STEPS + ADD_LAG):
             to_multiply = turn - MULTIPLY_LAG
@@ -259,13 +261,12 @@ def tile_gep_pb_t_kernel(tc, target_grad, embedding, bases0, bases1, bases2, out
                 square(to_square, 1)
             if 0 <= to_scale < STEPS:
                 scale(to_scale)
+                add_on_vector(to_scale)
             if turn < STEPS:
                 for bank in range(STEP_BANKS):
                     flip_bank(turn, bank)
-            if FIRST_SORTED_STEP <= turn + 1 < STEPS:
-                sort_bank(turn + 1)
             if 0 <= to_add < STEPS:
-                add_up(to_add)
+                add_on_tensor(to_add)
             if turn == 0:
                 flip_units(b_raw, b_grouped, 0, 2, False)
                 flip_units(b_raw, b_grouped, 2, 1, True)
@@ -273,8 +274,8 @@ def tile_gep_pb_t_kernel(tc, target_grad, embedding, bases0, bases1, bases2, out
                 quantise_units(b_grouped, b_codes, b_scales, 2, 1)
 
         nc.vector.tensor_reduce(out=totals[:, 0:GROUPS], in_=flipped_sums[:], axis=AXIS.X, op=ALU.add)
-        totals_flipped = flip_psum.tile([P, P], F32, tag="flipped")
-        nc.tensor.transpose(totals_flipped[:], totals[:], ident[:])
-        mean = const.tile([P, P], F32)
-        nc.scalar.mul(out=mean[:], in_=totals_flipped[:], mul=1.0 / BATCH)
-        nc.sync.dma_start(out=out.rearrange("(g j) -> g j", g=GROUPS), in_=mean[0:GROUPS, :])
+        rows = const.tile([P, BLOCK], F32, align_bytes=64)
+        nc.vector.transpose(out=rows[:], in_=totals[:])
+        out_rows = out.rearrange("(g q r) -> g q r", g=GROUPS, r=BLOCK)
+        for g in range(GROUPS):
+            nc.sync.dma_start(out=out_rows[g], in_=rows[g:P:BLOCK, :])

from contextlib import ExitStack

import concourse.mybir as mybir
from concourse.masks import make_identity

F32 = mybir.dt.float32
BF16 = mybir.dt.bfloat16
U32 = mybir.dt.uint32
U8 = mybir.dt.uint8
FP8X4 = mybir.dt.float8_e4m3fn_x4
ALU = mybir.AluOpType
ACT = mybir.ActivationFunctionType
AXIS = mybir.AxisListType

P = 128
BATCH = 4096
GROUPS = 3
K_GROUP = 512
K_ALL = GROUPS * K_GROUP
J_ALL = GROUPS * P
TILES = BATCH // P
STEP_TILES = 2
STEPS = TILES // STEP_TILES
LAST = STEPS - 1
STEP_UNITS = STEP_TILES * GROUPS
BLOCK = 32
UNIT_WORDS = K_GROUP // 2
BANK_UNITS = 2
STEP_BANKS = STEP_UNITS // BANK_UNITS
GRAD_FIRST_STEPS = (0, 2, 4, 8, 12)
VECTOR_COPY_BANK = 2
VECTOR_SUM_TILE = 0
DRAIN_STEPS = 3
QUANTISE_LAG = 1
MULTIPLY_LAG = 2
SQUARE_LAG = 3
SCALE_LAG = 4
ADD_LAG = 5

FLOPS = 2 * BATCH * K_ALL * P


def tile_gep_pb_t_kernel(tc, target_grad, embedding, bases0, bases1, bases2, out):
    nc = tc.nc
    with ExitStack() as ctx:
        ctx.enter_context(tc.manual_schedule())
        const = ctx.enter_context(tc.tile_pool(name="const", bufs=1))
        e_pool = ctx.enter_context(tc.tile_pool(name="e_pool", bufs=STEPS))
        g_pool = ctx.enter_context(tc.tile_pool(name="g_pool", bufs=len(GRAD_FIRST_STEPS)))
        grouped_pool = ctx.enter_context(tc.tile_pool(name="grouped_pool", bufs=3))
        mx_pool = ctx.enter_context(tc.tile_pool(name="mx_pool", bufs=3))
        resid_pool = ctx.enter_context(tc.tile_pool(name="resid_pool", bufs=ADD_LAG - MULTIPLY_LAG + 3))
        small_pool = ctx.enter_context(tc.tile_pool(name="small_pool", bufs=5))
        flip_psum = ctx.enter_context(tc.psum_pool(name="flip_psum", bufs=4))
        approx_psum = ctx.enter_context(tc.psum_pool(name="approx_psum", bufs=3))
        sums_psum = ctx.enter_context(tc.psum_pool(name="sums_psum", bufs=1))

        emb_rows = embedding.rearrange("(p t) k -> p (t k)", t=TILES)
        grad_rows = target_grad.rearrange("(p t) j -> p (t j)", t=TILES)
        b_raw = const.tile([P, K_ALL], BF16)
        e_raw = []
        g_raw = {}
        for s in range(STEPS):
            e_step = e_pool.tile([P, STEP_TILES * K_ALL], BF16)
            pieces = STEP_BANKS if s == 0 else 1
            piece = STEP_TILES * K_ALL // pieces
            for i in range(pieces):
                first = s * STEP_TILES * K_ALL + i * piece
                nc.sync.dma_start(out=e_step[:, i * piece : (i + 1) * piece], in_=emb_rows[:, first : first + piece])
            e_raw.append(e_step)
            if s == 0:
                for g, bases in enumerate((bases0, bases1, bases2)):
                    nc.sync.dma_start(out=b_raw[:, g * K_GROUP : (g + 1) * K_GROUP], in_=bases)
            if s - 1 in GRAD_FIRST_STEPS:
                load = GRAD_FIRST_STEPS.index(s - 1)
                end = GRAD_FIRST_STEPS[load + 1] if load + 1 < len(GRAD_FIRST_STEPS) else STEPS
                step_cols = STEP_TILES * J_ALL
                g_load = g_pool.tile([P, (end - s + 1) * step_cols], BF16)
                nc.sync.dma_start(out=g_load[:], in_=grad_rows[:, (s - 1) * step_cols : end * step_cols])
                for i in range(s - 1, end):
                    g_raw[i] = (g_load, (i - s + 1) * step_cols)

        ident = const.tile([P, P], F32)
        make_identity(nc, ident[:])
        sums = const.tile([P, J_ALL], F32)
        nc.vector.memset(sums[:], 0.0)
        totals = const.tile([P, BLOCK], F32, align_bytes=64)
        nc.vector.memset(totals[:], 0.0)
        warm = const.tile([P, 1], F32)
        nc.vector.memset(warm[:], 1.0)
        nc.scalar.activation(out=warm[:], in_=warm[:], func=ACT.Abs_reciprocal_sqrt)

        def flip_units(src, grouped, first_unit, n_units, on_vector):
            src_words = src[:].bitcast(F32)
            grouped_words = grouped[:].bitcast(F32)
            flipped = flip_psum.tile([P, BANK_UNITS, 2, P], F32)
            for n in range(n_units):
                for h in range(2):
                    unit_words = src_words[:, (first_unit + n) * UNIT_WORDS : (first_unit + n + 1) * UNIT_WORDS]
                    nc.tensor.transpose(flipped[:, n, h, :], unit_words[:, h : UNIT_WORDS : 2], ident[:])
            dst = grouped_words[:, first_unit * UNIT_WORDS : (first_unit + n_units) * UNIT_WORDS]
            dst = dst.rearrange("p (n r h) -> p n r h", n=n_units, h=2)
            flipped_rows = flipped[:, 0:n_units, :, :].rearrange("p n h r -> p n r h")
            if on_vector:
                nc.vector.tensor_copy(out=dst, in_=flipped_rows)
            else:
                nc.scalar.copy(out=dst, in_=flipped_rows)

        def quantise_units(grouped, codes, scales, first_unit, n_units):
            cols = slice(first_unit * P, (first_unit + n_units) * P)
            nc.vector.quantize_mx(
                out=codes[:, cols].bitcast(FP8X4),
                scales=scales[:, cols],
                in_=grouped[:, first_unit * K_GROUP : (first_unit + n_units) * K_GROUP],
            )

        b_grouped = const.tile([P, K_ALL], BF16, align_bytes=64)
        b_codes = const.tile([P, J_ALL], U32, align_bytes=64)
        b_scales = const.tile([P, J_ALL], U8, align_bytes=64)

        grouped_of = {}
        codes_of = {}
        scales_of = {}
        resid_of = {}
        sumsq_of = {}
        excess_of = {}
        factor_of = {}

        def flip_bank(s, bank):
            if bank == 0:
                grouped = grouped_pool.tile([P, STEP_UNITS * K_GROUP], BF16, align_bytes=64)
                grouped_of[s] = grouped
            on_vector = bank == VECTOR_COPY_BANK and s % 2 == 0
            flip_units(e_raw[s], grouped_of[s], bank * BANK_UNITS, BANK_UNITS, on_vector)

        def quantise(s, first_unit, n_units):
            if first_unit == 0:
                codes = mx_pool.tile([P, STEP_UNITS * P], U32, align_bytes=64)
                scales = mx_pool.tile([P, STEP_UNITS * P], U8, align_bytes=64)
                codes_of[s] = codes
                scales_of[s] = scales
            quantise_units(grouped_of[s], codes_of[s], scales_of[s], first_unit, n_units)

        def multiply(s):
            resid = resid_pool.tile([P, STEP_TILES * J_ALL], F32)
            resid_of[s] = resid
            for t in range(STEP_TILES):
                approx = approx_psum.tile([P, J_ALL], F32)
                for g in range(GROUPS):
                    unit_cols = slice((t * GROUPS + g) * P, (t * GROUPS + g + 1) * P)
                    g_cols = slice(g * P, (g + 1) * P)
                    nc.tensor.matmul_mx(
                        out=approx[:, g_cols],
                        lhsT=codes_of[s][:, unit_cols].bitcast(FP8X4),
                        lhsT_scale=scales_of[s][:, unit_cols],
                        rhs=b_codes[:, g_cols].bitcast(FP8X4),
                        rhs_scale=b_scales[:, g_cols],
                        start=True,
                        stop=True,
                    )
                g_load, g_first = g_raw[s]
                nc.vector.tensor_tensor(
                    out=resid[:, t * J_ALL : (t + 1) * J_ALL],
                    in0=g_load[:, g_first + t * J_ALL : g_first + (t + 1) * J_ALL],
                    in1=approx[:],
                    op=ALU.subtract,
                )

        def square(s, t):
            if t == 0:
                sumsq = small_pool.tile([P, STEP_TILES], F32)
                sumsq_of[s] = sumsq
            resid_t = resid_of[s][:, t * J_ALL : (t + 1) * J_ALL]
            squares = small_pool.tile([P, J_ALL], BF16)
            nc.scalar.activation(out=squares[:], in_=resid_t, func=ACT.Square, accum_out=sumsq_of[s][:, t : t + 1])

        def clip_excess(s):
            excess = small_pool.tile([P, STEP_TILES], F32)
            nc.scalar.activation(out=excess[:], in_=sumsq_of[s][:], func=ACT.Relu, bias=-1.0)
            excess_of[s] = excess

        def clip_factor(s):
            factor = small_pool.tile([P, STEP_TILES], F32)
            nc.scalar.activation(
                out=factor[:],
                in_=excess_of[s][:],
                func=ACT.Abs_reciprocal_sqrt,
                scale=float(BATCH**2),
                bias=float(BATCH**2),
            )
            factor_of[s] = factor

        def on_vector_sum(s, t):
            return t == VECTOR_SUM_TILE and s % 2 == 1 and s != LAST

        def scale(s):
            engine = nc.vector if s >= STEPS - DRAIN_STEPS else nc.gpsimd
            for t in range(STEP_TILES):
                if not on_vector_sum(s, t):
                    resid_t = resid_of[s][:, t * J_ALL : (t + 1) * J_ALL]
                    engine.tensor_scalar(
                        out=resid_t,
                        in0=resid_t,
                        scalar1=factor_of[s][:, t : t + 1],
                        scalar2=0.0,
                        op0=ALU.mult,
                        op1=ALU.add,
                    )

        def add_on_vector(s):
            for t in range(STEP_TILES):
                if on_vector_sum(s, t):
                    nc.vector.scalar_tensor_tensor(
                        out=sums[:],
                        in0=resid_of[s][:, t * J_ALL : (t + 1) * J_ALL],
                        scalar=factor_of[s][:, t : t + 1],
                        in1=sums[:],
                        op0=ALU.mult,
                        op1=ALU.add,
                    )

        flipped_sums = sums_psum.tile([P, GROUPS, P], F32)

        def add_flipped(src, first_col, start, stop):
            for g in range(GROUPS):
                nc.tensor.matmul(
                    out=flipped_sums[:, g, :],
                    lhsT=src[:, first_col + g * P : first_col + (g + 1) * P],
                    rhs=ident[:],
                    is_transpose=True,
                    start=start and g == 0,
                    stop=stop and g == GROUPS - 1,
                )

        def add_on_tensor(s):
            if s == LAST:
                add_flipped(sums, 0, False, False)
            for t in range(STEP_TILES):
                if not on_vector_sum(s, t):
                    tile_index = s * STEP_TILES + t
                    add_flipped(resid_of[s], t * J_ALL, tile_index == 0, tile_index == TILES - 1)

        for turn in range(STEPS + ADD_LAG):
            to_multiply = turn - MULTIPLY_LAG
            to_quantise = turn - QUANTISE_LAG
            to_square = turn - SQUARE_LAG
            to_scale = turn - SCALE_LAG
            to_add = turn - ADD_LAG
            if 0 <= to_quantise < STEPS:
                quantise(to_quantise, 0, BANK_UNITS)
                quantise(to_quantise, BANK_UNITS, STEP_UNITS - BANK_UNITS)
            if 0 <= to_multiply < STEPS:
                multiply(to_multiply)
            if 0 <= to_scale < STEPS:
                clip_excess(to_scale)
            if 0 <= to_square < STEPS:
                square(to_square, 0)
            if 0 <= to_scale < STEPS:
                clip_factor(to_scale)
            if 0 <= to_square < STEPS:
                square(to_square, 1)
            if 0 <= to_scale < STEPS:
                scale(to_scale)
                add_on_vector(to_scale)
            if turn < STEPS:
                for bank in range(STEP_BANKS):
                    flip_bank(turn, bank)
            if 0 <= to_add < STEPS:
                add_on_tensor(to_add)
            if turn == 0:
                flip_units(b_raw, b_grouped, 0, 2, False)
                flip_units(b_raw, b_grouped, 2, 1, True)
                quantise_units(b_grouped, b_codes, b_scales, 0, 2)
                quantise_units(b_grouped, b_codes, b_scales, 2, 1)

        nc.vector.tensor_reduce(out=totals[:, 0:GROUPS], in_=flipped_sums[:], axis=AXIS.X, op=ALU.add)
        rows = const.tile([P, BLOCK], F32, align_bytes=64)
        nc.vector.transpose(out=rows[:], in_=totals[:])
        out_rows = out.rearrange("(g q r) -> g q r", g=GROUPS, r=BLOCK)
        for g in range(GROUPS):
            nc.sync.dma_start(out=out_rows[g], in_=rows[g:P:BLOCK, :])
